import numpy as np
import ml_dtypes


def mxq(x, axis, fmt="e4m3"):
    dtype, down = {"e4m3": (ml_dtypes.float8_e4m3fn, 7), "e5m2": (ml_dtypes.float8_e5m2, 14)}[fmt]
    v = np.moveaxis(np.asarray(x, np.float32).astype(ml_dtypes.bfloat16).astype(np.float64), axis, -1)
    blocks = v.reshape(v.shape[:-1] + (-1, 32))
    amax = np.abs(blocks).max(-1, keepdims=True)
    byte = np.maximum(np.where(amax > 0, np.frexp(amax)[1] - 1 + 127, 0) - down, 1)
    scale = np.exp2(byte - 127.0)
    codes = (blocks / scale).astype(np.float32).astype(dtype).astype(np.float64)
    return np.moveaxis((codes * scale).reshape(v.shape), -1, axis)


WIDE = False


def mx_kscale(k):
    if not WIDE:
        return np.ones(k)
    levels = np.array([10, -10, 5, -5, 0])
    a = np.random.permutation(np.resize(levels, k // 512 * 4)).reshape(k // 512, 4)
    idx = np.arange(k)
    return np.exp2(a[idx // 512, idx % 128 // 32])


BF16 = ml_dtypes.bfloat16


def bf(x):
    return np.asarray(x, np.float32).astype(BF16)


def f64(x):
    return np.asarray(x).astype(np.float64)


E2M1 = np.array([0.0, 0.5, 1.0, 1.5, 2.0, 3.0, 4.0, 6.0, -0.0, -0.5, -1.0, -1.5, -2.0, -3.0, -4.0, -6.0])


def pack_weight(w, fmt):
    k, n = w.shape
    w = f64(bf(w)).reshape(k // 32, 32, n)
    amax = np.abs(w).max(1)
    if fmt == "e4m3":
        byte = np.frexp(amax)[1] - 1 + 127 - 7
    else:
        mant, ex = np.frexp(amax / 6.0)
        byte = np.where(mant > 0.5, ex, ex - 1) + 127
    byte = np.clip(np.where(amax > 0, byte, 1), 1, 254)
    scaled = (w * np.exp2(127.0 - byte)[:, None, :]).reshape(k, n).astype(np.float32)
    by_word = np.ascontiguousarray(scaled.reshape(k // 512, 128, 4, n).transpose(0, 1, 3, 2))
    if fmt == "e4m3":
        words = by_word.astype(ml_dtypes.float8_e4m3fn).view(np.uint8)
    else:
        c = by_word.astype(ml_dtypes.float4_e2m1fn).view(np.uint8) & 0xF
        words = c[..., 0::2] | (c[..., 1::2] << 4)
    return np.ascontiguousarray(words), np.ascontiguousarray(byte.astype(np.uint8).reshape(k // 512, 16, n))


def unpack_weight(words, scales, fmt):
    g, p, n, _ = words.shape
    if fmt == "e4m3":
        vals = np.ascontiguousarray(words).view(ml_dtypes.float8_e4m3fn).astype(np.float64)
    else:
        nib = np.empty((g, p, n, 4), np.uint8)
        nib[..., 0::2] = words & 0xF
        nib[..., 1::2] = words >> 4
        vals = E2M1[nib]
    vals = vals * np.repeat(np.exp2(scales.astype(np.float64) - 127.0), 8, axis=1)[..., None]
    return vals.transpose(0, 1, 3, 2).reshape(g * 512, n)


B, S, D, H, HD, FF = 1, 128, 8192, 8, 128, 2560
E = H * HD
EPS = 1e-6


def rmsnorm(x, g):
    return x * (1.0 / np.sqrt(np.mean(x * x, axis=-1, keepdims=True) + EPS)) * g


def rotate_half(x):
    x1, x2 = np.split(x, 2, axis=-1)
    return np.concatenate([-x2, x1], axis=-1)


def rope(x, cos, sin):
    return x * cos + rotate_half(x) * sin


def setup_inputs():
    s = mx_kscale(D)
    inv_freq = 1.0 / (10000.0 ** (np.arange(0, HD, 2) / HD))
    freqs = np.arange(S)[:, None] * inv_freq[None, :]
    emb = np.concatenate([freqs, freqs], axis=-1)
    hidden_states = bf(np.random.standard_normal((B, S, D)))
    cos = bf(np.cos(emb)[None, :, None, :])
    sin = bf(np.sin(emb)[None, :, None, :])
    g1 = bf((1.0 + 0.1 * np.random.standard_normal(D)) * s)
    words, scales = pack_weight(np.random.standard_normal((D, 3 * E)) / np.sqrt(D) / s[:, None], "e4m3")
    bqkv = bf(0.2 * np.random.standard_normal(3 * E))
    return {"hidden_states": hidden_states,
            "cos": cos,
            "sin": sin,
            "g1": g1,
            "Wqkv_words": words,
            "Wqkv_scales": scales,
            "bqkv": bqkv}


def reference(hidden_states, cos, sin, g1, Wqkv_words, Wqkv_scales, bqkv):
    x = rmsnorm(f64(hidden_states), f64(g1))
    qkv = (mxq(x, 2, "e4m3") @ unpack_weight(Wqkv_words, Wqkv_scales, "e4m3")) + f64(bqkv)
    q, k, v = np.split(qkv, 3, axis=-1)
    q = q.reshape(B, S, H, HD)
    k = k.reshape(B, S, H, HD)
    v = v.reshape(B, S, H, HD)
    return rope(q, f64(cos), f64(sin)), rope(k, f64(cos), f64(sin)), v

@@ -1,0 +1,226 @@
+from contextlib import ExitStack
+
+import concourse.masks as masks
+import concourse.mybir as mybir
+
+F32 = mybir.dt.float32
+BF16 = mybir.dt.bfloat16
+I32 = mybir.dt.int32
+U32 = mybir.dt.uint32
+U8 = mybir.dt.uint8
+FP8X4 = mybir.dt.float8_e4m3fn_x4
+ALU = mybir.AluOpType
+ACT = mybir.ActivationFunctionType
+
+P = 128
+PACK = 4
+K_PASS = P * PACK
+D = 8192
+GROUPS = D // K_PASS
+HEADS = 8
+HEAD_DIM = 128
+HALF = HEAD_DIM // 2
+PART = HEADS * HEAD_DIM
+N_OUT = 3 * PART
+BANK = 512
+QK_BANKS = 2 * PART // BANK
+V_BANKS = PART // BANK
+X_CHUNK = 2048
+SHARE = 4
+EPS = 1e-6
+
+FLOPS = 2 * P * D * N_OUT
+
+
+def tile_qwenblock_pa_k_kernel(
+    tc, hidden_states, cos, sin, g1, Wqkv_words, Wqkv_scales, bqkv, out_0, out_1, out_2
+):
+    nc = tc.nc
+    with ExitStack() as ctx:
+        ctx.enter_context(tc.manual_schedule())
+        keep = ctx.enter_context(tc.tile_pool(name="keep", bufs=1))
+        squares = ctx.enter_context(tc.tile_pool(name="squares", bufs=2))
+        stage = ctx.enter_context(tc.tile_pool(name="stage", bufs=3))
+        quant = ctx.enter_context(tc.tile_pool(name="quant", bufs=2))
+        w_qk_pool = ctx.enter_context(tc.tile_pool(name="w_qk", bufs=8))
+        w_v_pool = ctx.enter_context(tc.tile_pool(name="w_v", bufs=8))
+        result = ctx.enter_context(tc.tile_pool(name="result", bufs=2))
+        psum_acc = ctx.enter_context(tc.psum_pool(name="psum_acc", bufs=1))
+        psum_work = ctx.enter_context(tc.psum_pool(name="psum_work", bufs=2))
+
+        h_sb = keep.tile([P, D], BF16)
+        g1_rows = keep.tile([P, K_PASS], BF16)
+        g1_sorted = keep.tile([P, PACK, P], BF16)
+        g1_t = keep.tile([P, GROUPS, PACK], F32)
+        bias_rows = keep.tile([P, N_OUT], BF16)
+        bias_all = keep.tile([P, N_OUT], F32)
+        cos_sb = keep.tile([P, HEAD_DIM], BF16)
+        sin_sb = keep.tile([P, HEAD_DIM], BF16)
+        sin_signed = keep.tile([P, HEAD_DIM], BF16)
+        ident_f32 = keep.tile([P, P], F32)
+        ident_bf16 = keep.tile([P, P], BF16)
+        ones_bf16 = keep.tile([P, P], BF16)
+        one_col = keep.tile([P, 1], F32)
+        warm_col = keep.tile([P, 1], F32)
+        sum_sq = keep.tile([P, D // X_CHUNK], F32)
+        sum_sq_all = keep.tile([P, 1], F32)
+        mean_sq = keep.tile([P, 1], F32)
+        rms = keep.tile([P, 1], F32)
+        inv_rms = keep.tile([P, 1], F32)
+        x_codes = keep.tile([P, GROUPS, P], U32, align_bytes=64)
+        x_planes = keep.tile([P, GROUPS, P], U8, align_bytes=64)
+        w_planes = keep.tile([P, GROUPS // SHARE, N_OUT], U8, align_bytes=64)
+        acc = [psum_acc.tile([P, BANK], F32, name="acc%d" % b) for b in range(QK_BANKS + V_BANKS)]
+
+        nc.vector.memset(g1_rows[:], 0.0)
+        nc.vector.memset(bias_rows[:], 0.0)
+        nc.vector.memset(w_planes[:].bitcast(I32), 0)
+        nc.vector.memset(one_col[:], 1.0)
+        masks.make_identity(nc, ident_bf16[:])
+        masks.make_identity(nc, ident_f32[:])
+        nc.gpsimd.memset(ones_bf16[:], 1.0)
+        nc.scalar.activation(out=warm_col[:], in_=one_col[:], func=ACT.Sqrt)
+
+        h_flat = hidden_states.flatten_outer_dims()
+        for c in range(D // X_CHUNK):
+            cols = slice(c * X_CHUNK, (c + 1) * X_CHUNK)
+            nc.sync.dma_start(out=h_sb[:, cols], in_=h_flat[:, cols])
+        nc.sync.dma_start(out=g1_rows[0:GROUPS, :], in_=g1.rearrange("(g c) -> g c", c=K_PASS))
+        nc.sync.dma_start(out=bias_rows[0:1, :], in_=bqkv.rearrange("(o n) -> o n", o=1))
+        nc.sync.dma_start(out=cos_sb[:], in_=cos.rearrange("b s o d -> (b s o) d"))
+        nc.sync.dma_start(out=sin_sb[:], in_=sin.rearrange("b s o d -> (b s o) d"))
+        for j in range(GROUPS // SHARE):
+            for quadrant in range(4):
+                nc.sync.dma_start(
+                    out=w_planes[32 * quadrant : 32 * quadrant + 4 * SHARE, j, :].bitcast(I32),
+                    in_=Wqkv_scales[
+                        SHARE * j : SHARE * (j + 1), 4 * quadrant : 4 * quadrant + 4, :
+                    ].bitcast(I32),
+                )
+
+        nc.vector.tensor_copy(out=g1_sorted[:], in_=g1_rows[:].rearrange("r (p t) -> r t p", t=PACK))
+        g1_ps = psum_work.tile([P, PACK, P], BF16, tag="work")
+        for t in range(PACK):
+            nc.tensor.transpose(g1_ps[:, t, :], g1_sorted[:, t, :], ident_bf16[:])
+        nc.vector.tensor_copy(out=g1_t[:], in_=g1_ps[:, :, 0:GROUPS].rearrange("p t g -> p g t"))
+
+        for b in range(QK_BANKS + V_BANKS):
+            cols = slice(b * BANK, (b + 1) * BANK)
+            bias_ps = psum_work.tile([P, BANK], F32, tag="work")
+            nc.tensor.matmul(out=bias_ps[:], lhsT=ones_bf16[:], rhs=bias_rows[:, cols], start=True, stop=True)
+            nc.vector.tensor_copy(out=bias_all[:, cols], in_=bias_ps[:])
+
+        nc.vector.tensor_scalar_mul(out=sin_signed[:, 0:HALF], in0=sin_sb[:, 0:HALF], scalar1=-1.0)
+        nc.vector.tensor_copy(out=sin_signed[:, HALF:HEAD_DIM], in_=sin_sb[:, HALF:HEAD_DIM])
+
+        for c in range(D // X_CHUNK):
+            cols = slice(c * X_CHUNK, (c + 1) * X_CHUNK)
+            squared = squares.tile([P, X_CHUNK], BF16)
+            nc.scalar.activation(
+                out=squared[:], in_=h_sb[:, cols], func=ACT.Square, accum_out=sum_sq[:, c : c + 1]
+            )
+        nc.vector.tensor_reduce(out=sum_sq_all[:], in_=sum_sq[:], axis=mybir.AxisListType.X, op=ALU.add)
+        nc.vector.tensor_scalar(
+            out=mean_sq[:], in0=sum_sq_all[:], scalar1=1.0 / D, scalar2=EPS, op0=ALU.mult, op1=ALU.add
+        )
+        nc.scalar.activation(out=rms[:], in_=mean_sq[:], func=ACT.Sqrt)
+        nc.vector.reciprocal(out=inv_rms[:], in_=rms[:])
+
+        def quantise_x(first_group):
+            grouped = quant.tile([P, SHARE, P, PACK], BF16, align_bytes=64)
+            for s in range(SHARE):
+                g = first_group + s
+                scaled = stage.tile([P, PACK, P], F32)
+                nc.scalar.activation(
+                    out=scaled[:],
+                    in_=h_sb[:, g * K_PASS : (g + 1) * K_PASS].rearrange("m (p t) -> m t p", t=PACK),
+                    func=ACT.Copy,
+                    scale=inv_rms[:, 0:1],
+                )
+                turned = psum_work.tile([P, PACK, P], F32, tag="work")
+                for t in range(PACK):
+                    nc.tensor.transpose(turned[:, t, :], scaled[:, t, :], ident_f32[:])
+                nc.vector.tensor_tensor(
+                    out=grouped[:, s, :, :],
+                    in0=turned[:].rearrange("p t m -> p m t"),
+                    in1=g1_t[:, g, :].unsqueeze(1).to_broadcast([P, P, PACK]),
+                    op=ALU.mult,
+                )
+            groups = slice(first_group, first_group + SHARE)
+            nc.vector.quantize_mx(
+                out=x_codes[:, groups, :].rearrange("p g m -> p (g m)").bitcast(FP8X4),
+                scales=x_planes[:, groups, :].rearrange("p g m -> p (g m)"),
+                in_=grouped[:].rearrange("p g m t -> p (g m t)"),
+            )
+
+        def load_words(pool, g, first_bank, banks):
+            words = pool.tile([P, banks * BANK], U32, align_bytes=64, tag="words")
+            byte_cols = slice(first_bank * BANK * PACK, (first_bank + banks) * BANK * PACK)
+            nc.sync.dma_start(
+                out=words[:].bitcast(I32),
+                in_=Wqkv_words[g].rearrange("p n t -> p (n t)")[:, byte_cols].bitcast(I32),
+            )
+            return words
+
+        def multiply(g, words, first_bank, banks):
+            for i in range(banks):
+                b = first_bank + i
+                nc.tensor.matmul_mx(
+                    out=acc[b][:],
+                    lhsT=x_codes[:, g, :].bitcast(FP8X4),
+                    lhsT_scale=x_planes[:, g, :],
+                    rhs=words[:, i * BANK : (i + 1) * BANK].bitcast(FP8X4),
+                    rhs_scale=w_planes[4 * (g % SHARE) : P, g // SHARE, b * BANK : (b + 1) * BANK],
+                    start=(g == 0),
+                    stop=(g == GROUPS - 1),
+                )
+
+        def rope_and_store(first_bank, out):
+            u = result.tile([P, HEADS, HEAD_DIM], F32)
+            swapped = result.tile([P, HEADS, HEAD_DIM], F32)
+            heads_in_bank = BANK // HEAD_DIM
+            for i in range(PART // BANK):
+                b = first_bank + i
+                nc.vector.tensor_tensor(
+                    out=u[:, i * heads_in_bank : (i + 1) * heads_in_bank, :],
+                    in0=acc[b][:].rearrange("m (h d) -> m h d", d=HEAD_DIM),
+                    in1=bias_all[:, b * BANK : (b + 1) * BANK].rearrange("m (h d) -> m h d", d=HEAD_DIM),
+                    op=ALU.add,
+                )
+            nc.vector.tensor_tensor(
+                out=swapped[:, :, 0:HALF],
+                in0=u[:, :, HALF:HEAD_DIM],
+                in1=sin_signed[:, 0:HALF].unsqueeze(1).to_broadcast([P, HEADS, HALF]),
+                op=ALU.mult,
+            )
+            nc.vector.tensor_tensor(
+                out=swapped[:, :, HALF:HEAD_DIM],
+                in0=u[:, :, 0:HALF],
+                in1=sin_signed[:, HALF:HEAD_DIM].unsqueeze(1).to_broadcast([P, HEADS, HALF]),
+                op=ALU.mult,
+            )
+            nc.vector.tensor_tensor(
+                out=u[:], in0=u[:], in1=cos_sb[:].unsqueeze(1).to_broadcast([P, HEADS, HEAD_DIM]), op=ALU.mult
+            )
+            nc.vector.tensor_tensor(out=u[:], in0=u[:], in1=swapped[:], op=ALU.add)
+            nc.scalar.dma_start(out=out.rearrange("b s h d -> (b s) h d"), in_=u[:])
+
+        for first_group in range(0, GROUPS, SHARE):
+            quantise_x(first_group)
+            for g in range(first_group, first_group + SHARE):
+                words = load_words(w_qk_pool, g, 0, QK_BANKS)
+                multiply(g, words, 0, QK_BANKS)
+        rope_and_store(0, out_0)
+        rope_and_store(PART // BANK, out_1)
+
+        for g in range(GROUPS):
+            words = load_words(w_v_pool, g, QK_BANKS, V_BANKS)
+            multiply(g, words, QK_BANKS, V_BANKS)
+        v_flat = out_2.rearrange("b s h d -> (b s) (h d)")
+        for i in range(V_BANKS):
+            b = QK_BANKS + i
+            v_sb = result.tile([P, BANK], F32)
+            nc.vector.tensor_tensor(
+                out=v_sb[:], in0=acc[b][:], in1=bias_all[:, b * BANK : (b + 1) * BANK], op=ALU.add
+            )
+            nc.sync.dma_start(out=v_flat[:, i * BANK : (i + 1) * BANK], in_=v_sb[:])

@@ -27,6 +27,7 @@ QK_BANKS = 2 * PART // BANK
 V_BANKS = PART // BANK
 X_CHUNK = 2048
 SHARE = 4
+AHEAD = 4
 EPS = 1e-6
 
 FLOPS = 2 * P * D * N_OUT
@@ -41,7 +42,7 @@ def tile_qwenblock_pa_k_kernel(
         keep = ctx.enter_context(tc.tile_pool(name="keep", bufs=1))
         squares = ctx.enter_context(tc.tile_pool(name="squares", bufs=2))
         stage = ctx.enter_context(tc.tile_pool(name="stage", bufs=3))
-        quant = ctx.enter_context(tc.tile_pool(name="quant", bufs=2))
+        quant = ctx.enter_context(tc.tile_pool(name="quant", bufs=3))
         w_qk_pool = ctx.enter_context(tc.tile_pool(name="w_qk", bufs=8))
         w_v_pool = ctx.enter_context(tc.tile_pool(name="w_v", bufs=8))
         result = ctx.enter_context(tc.tile_pool(name="result", bufs=2))
@@ -126,31 +127,28 @@ def tile_qwenblock_pa_k_kernel(
         nc.scalar.activation(out=rms[:], in_=mean_sq[:], func=ACT.Sqrt)
         nc.vector.reciprocal(out=inv_rms[:], in_=rms[:])
 
-        def quantise_x(first_group):
-            grouped = quant.tile([P, SHARE, P, PACK], BF16, align_bytes=64)
-            for s in range(SHARE):
-                g = first_group + s
-                scaled = stage.tile([P, PACK, P], F32)
-                nc.scalar.activation(
-                    out=scaled[:],
-                    in_=h_sb[:, g * K_PASS : (g + 1) * K_PASS].rearrange("m (p t) -> m t p", t=PACK),
-                    func=ACT.Copy,
-                    scale=inv_rms[:, 0:1],
-                )
-                turned = psum_work.tile([P, PACK, P], F32, tag="work")
-                for t in range(PACK):
-                    nc.tensor.transpose(turned[:, t, :], scaled[:, t, :], ident_f32[:])
-                nc.vector.tensor_tensor(
-                    out=grouped[:, s, :, :],
-                    in0=turned[:].rearrange("p t m -> p m t"),
-                    in1=g1_t[:, g, :].unsqueeze(1).to_broadcast([P, P, PACK]),
-                    op=ALU.mult,
-                )
-            groups = slice(first_group, first_group + SHARE)
+        def quantise_x(g):
+            scaled = stage.tile([P, PACK, P], F32)
+            nc.scalar.activation(
+                out=scaled[:],
+                in_=h_sb[:, g * K_PASS : (g + 1) * K_PASS].rearrange("m (p t) -> m t p", t=PACK),
+                func=ACT.Copy,
+                scale=inv_rms[:, 0:1],
+            )
+            turned = psum_work.tile([P, PACK, P], F32, tag="work")
+            for t in range(PACK):
+                nc.tensor.transpose(turned[:, t, :], scaled[:, t, :], ident_f32[:])
+            grouped = quant.tile([P, P, PACK], BF16, align_bytes=64)
+            nc.vector.tensor_tensor(
+                out=grouped[:],
+                in0=turned[:].rearrange("p t m -> p m t"),
+                in1=g1_t[:, g, :].unsqueeze(1).to_broadcast([P, P, PACK]),
+                op=ALU.mult,
+            )
             nc.vector.quantize_mx(
-                out=x_codes[:, groups, :].rearrange("p g m -> p (g m)").bitcast(FP8X4),
-                scales=x_planes[:, groups, :].rearrange("p g m -> p (g m)"),
-                in_=grouped[:].rearrange("p g m t -> p (g m t)"),
+                out=x_codes[:, g, :].bitcast(FP8X4),
+                scales=x_planes[:, g, :],
+                in_=grouped[:].rearrange("p m t -> p (m t)"),
             )
 
         def load_words(pool, g, first_bank, banks):
@@ -205,11 +203,13 @@ def tile_qwenblock_pa_k_kernel(
             nc.vector.tensor_tensor(out=u[:], in0=u[:], in1=swapped[:], op=ALU.add)
             nc.scalar.dma_start(out=out.rearrange("b s h d -> (b s) h d"), in_=u[:])
 
-        for first_group in range(0, GROUPS, SHARE):
-            quantise_x(first_group)
-            for g in range(first_group, first_group + SHARE):
-                words = load_words(w_qk_pool, g, 0, QK_BANKS)
-                multiply(g, words, 0, QK_BANKS)
+        for g in range(AHEAD):
+            quantise_x(g)
+        for g in range(GROUPS):
+            words = load_words(w_qk_pool, g, 0, QK_BANKS)
+            multiply(g, words, 0, QK_BANKS)
+            if g + AHEAD < GROUPS:
+                quantise_x(g + AHEAD)
         rope_and_store(0, out_0)
         rope_and_store(PART // BANK, out_1)
 

@@ -73,10 +73,10 @@ def tile_qwenblock_pa_k_kernel(
         w_planes = keep.tile([P, GROUPS // SHARE, N_OUT], U8, align_bytes=64)
         acc = [psum_acc.tile([P, BANK], F32, name="acc%d" % b) for b in range(QK_BANKS + V_BANKS)]
 
+        nc.vector.memset(one_col[:], 1.0)
         nc.vector.memset(g1_rows[:], 0.0)
         nc.vector.memset(bias_rows[:], 0.0)
         nc.vector.memset(w_planes[:].bitcast(I32), 0)
-        nc.vector.memset(one_col[:], 1.0)
         masks.make_identity(nc, ident_bf16[:])
         masks.make_identity(nc, ident_f32[:])
         nc.gpsimd.memset(ones_bf16[:], 1.0)
@@ -86,17 +86,17 @@ def tile_qwenblock_pa_k_kernel(
         for c in range(D // X_CHUNK):
             cols = slice(c * X_CHUNK, (c + 1) * X_CHUNK)
             nc.sync.dma_start(out=h_sb[:, cols], in_=h_flat[:, cols])
-        nc.sync.dma_start(out=g1_rows[0:GROUPS, :], in_=g1.rearrange("(g c) -> g c", c=K_PASS))
-        nc.sync.dma_start(out=bias_rows[0:1, :], in_=bqkv.rearrange("(o n) -> o n", o=1))
-        nc.sync.dma_start(out=cos_sb[:], in_=cos.rearrange("b s o d -> (b s o) d"))
-        nc.sync.dma_start(out=sin_sb[:], in_=sin.rearrange("b s o d -> (b s o) d"))
+        nc.scalar.dma_start(out=g1_rows[0:GROUPS, :], in_=g1.rearrange("(g c) -> g c", c=K_PASS))
+        nc.scalar.dma_start(out=bias_rows[0:1, :], in_=bqkv.rearrange("(o n) -> o n", o=1))
+        nc.scalar.dma_start(out=cos_sb[:], in_=cos.rearrange("b s o d -> (b s o) d"))
+        nc.scalar.dma_start(out=sin_sb[:], in_=sin.rearrange("b s o d -> (b s o) d"))
         for j in range(GROUPS // SHARE):
             for quadrant in range(4):
-                nc.sync.dma_start(
-                    out=w_planes[32 * quadrant : 32 * quadrant + 4 * SHARE, j, :].bitcast(I32),
+                nc.gpsimd.dma_start(
+                    out=w_planes[32 * quadrant : 32 * quadrant + 4 * SHARE, j, :].bitcast(F32),
                     in_=Wqkv_scales[
                         SHARE * j : SHARE * (j + 1), 4 * quadrant : 4 * quadrant + 4, :
-                    ].bitcast(I32),
+                    ].bitcast(F32),
                 )
 
         nc.vector.tensor_copy(out=g1_sorted[:], in_=g1_rows[:].rearrange("r (p t) -> r t p", t=PACK))

@@ -201,7 +201,7 @@ def tile_qwenblock_pa_k_kernel(
                 out=u[:], in0=u[:], in1=cos_sb[:].unsqueeze(1).to_broadcast([P, HEADS, HEAD_DIM]), op=ALU.mult
             )
             nc.vector.tensor_tensor(out=u[:], in0=u[:], in1=swapped[:], op=ALU.add)
-            nc.scalar.dma_start(out=out.rearrange("b s h d -> (b s) h d"), in_=u[:])
+            return u
 
         for g in range(AHEAD):
             quantise_x(g)
@@ -210,12 +210,14 @@ def tile_qwenblock_pa_k_kernel(
             multiply(g, words, 0, QK_BANKS)
             if g + AHEAD < GROUPS:
                 quantise_x(g + AHEAD)
-        rope_and_store(0, out_0)
-        rope_and_store(PART // BANK, out_1)
+        q_sb = rope_and_store(0, out_0)
+        k_sb = rope_and_store(PART // BANK, out_1)
 
         for g in range(GROUPS):
             words = load_words(w_v_pool, g, QK_BANKS, V_BANKS)
             multiply(g, words, QK_BANKS, V_BANKS)
+        nc.sync.dma_start(out=out_0.rearrange("b s h d -> (b s) h d"), in_=q_sb[:])
+        nc.sync.dma_start(out=out_1.rearrange("b s h d -> (b s) h d"), in_=k_sb[:])
         v_flat = out_2.rearrange("b s h d -> (b s) (h d)")
         for i in range(V_BANKS):
             b = QK_BANKS + i

@@ -28,6 +28,7 @@ V_BANKS = PART // BANK
 X_CHUNK = 2048
 SHARE = 4
 AHEAD = 4
+TAIL = 256
 EPS = 1e-6
 
 FLOPS = 2 * P * D * N_OUT
@@ -151,26 +152,29 @@ def tile_qwenblock_pa_k_kernel(
                 in_=grouped[:].rearrange("p m t -> p (m t)"),
             )
 
-        def load_words(pool, g, first_bank, banks):
-            words = pool.tile([P, banks * BANK], U32, align_bytes=64, tag="words")
-            byte_cols = slice(first_bank * BANK * PACK, (first_bank + banks) * BANK * PACK)
+        def load_columns(pool, g, first_col, cols):
+            words = pool.tile([P, cols], U32, align_bytes=64, tag="words")
+            byte_cols = slice(first_col * PACK, (first_col + cols) * PACK)
             nc.sync.dma_start(
                 out=words[:].bitcast(I32),
                 in_=Wqkv_words[g].rearrange("p n t -> p (n t)")[:, byte_cols].bitcast(I32),
             )
             return words
 
-        def multiply(g, words, first_bank, banks):
+        def load_words(pool, g, first_bank, banks):
+            return load_columns(pool, g, first_bank * BANK, banks * BANK)
+
+        def multiply(g, words, first_bank, banks, skip=0, last_group=GROUPS - 1):
             for i in range(banks):
                 b = first_bank + i
                 nc.tensor.matmul_mx(
                     out=acc[b][:],
                     lhsT=x_codes[:, g, :].bitcast(FP8X4),
                     lhsT_scale=x_planes[:, g, :],
-                    rhs=words[:, i * BANK : (i + 1) * BANK].bitcast(FP8X4),
+                    rhs=words[:, (skip + i) * BANK : (skip + i + 1) * BANK].bitcast(FP8X4),
                     rhs_scale=w_planes[4 * (g % SHARE) : P, g // SHARE, b * BANK : (b + 1) * BANK],
                     start=(g == 0),
-                    stop=(g == GROUPS - 1),
+                    stop=(g == last_group),
                 )
 
         def rope_and_store(first_bank, out):
@@ -213,16 +217,40 @@ def tile_qwenblock_pa_k_kernel(
         q_sb = rope_and_store(0, out_0)
         k_sb = rope_and_store(PART // BANK, out_1)
 
-        for g in range(GROUPS):
+        last = GROUPS - 1
+        bank_a, bank_b = QK_BANKS, QK_BANKS + 1
+        for g in range(last):
             words = load_words(w_v_pool, g, QK_BANKS, V_BANKS)
-            multiply(g, words, QK_BANKS, V_BANKS)
+            multiply(g, words, bank_a, 1)
+            multiply(g, words, bank_b, 1, skip=1, last_group=last - 1)
+        words = load_words(w_v_pool, last, bank_a, 1)
+        multiply(last, words, bank_a, 1)
+        late = []
+        for i in range(BANK // TAIL):
+            first_col = bank_b * BANK + i * TAIL
+            words = load_columns(w_v_pool, last, first_col, TAIL)
+            late_ps = psum_work.tile([P, TAIL], F32, tag="work")
+            nc.tensor.matmul_mx(
+                out=late_ps[:],
+                lhsT=x_codes[:, last, :].bitcast(FP8X4),
+                lhsT_scale=x_planes[:, last, :],
+                rhs=words[:].bitcast(FP8X4),
+                rhs_scale=w_planes[4 * (last % SHARE) : P, last // SHARE, first_col : first_col + TAIL],
+                start=True,
+                stop=True,
+            )
+            late.append(late_ps)
         nc.sync.dma_start(out=out_0.rearrange("b s h d -> (b s) h d"), in_=q_sb[:])
         nc.sync.dma_start(out=out_1.rearrange("b s h d -> (b s) h d"), in_=k_sb[:])
         v_flat = out_2.rearrange("b s h d -> (b s) (h d)")
-        for i in range(V_BANKS):
-            b = QK_BANKS + i
-            v_sb = result.tile([P, BANK], F32)
+        v_sb = {}
+        for b in (bank_b, bank_a):
+            v_sb[b] = result.tile([P, BANK], F32, name="v_sb%d" % b)
             nc.vector.tensor_tensor(
-                out=v_sb[:], in0=acc[b][:], in1=bias_all[:, b * BANK : (b + 1) * BANK], op=ALU.add
+                out=v_sb[b][:], in0=acc[b][:], in1=bias_all[:, b * BANK : (b + 1) * BANK], op=ALU.add
             )
-            nc.sync.dma_start(out=v_flat[:, i * BANK : (i + 1) * BANK], in_=v_sb[:])
+        nc.sync.dma_start(out=v_flat[:, 0:BANK], in_=v_sb[bank_a][:])
+        for i in range(BANK // TAIL):
+            cols = slice(i * TAIL, (i + 1) * TAIL)
+            nc.vector.tensor_tensor(out=v_sb[bank_b][:, cols], in0=late[i][:], in1=v_sb[bank_b][:, cols], op=ALU.add)
+            nc.sync.dma_start(out=v_flat[:, BANK + i * TAIL : BANK + (i + 1) * TAIL], in_=v_sb[bank_b][:, cols])

@@ -26,9 +26,11 @@ BANK = 512
 QK_BANKS = 2 * PART // BANK
 V_BANKS = PART // BANK
 X_CHUNK = 2048
+X_LOAD = 4096
 SHARE = 4
 AHEAD = 4
 TAIL = 256
+FULL_GROUPS = 6
 EPS = 1e-6
 
 FLOPS = 2 * P * D * N_OUT
@@ -44,8 +46,7 @@ def tile_qwenblock_pa_k_kernel(
         squares = ctx.enter_context(tc.tile_pool(name="squares", bufs=2))
         stage = ctx.enter_context(tc.tile_pool(name="stage", bufs=3))
         quant = ctx.enter_context(tc.tile_pool(name="quant", bufs=3))
-        w_qk_pool = ctx.enter_context(tc.tile_pool(name="w_qk", bufs=8))
-        w_v_pool = ctx.enter_context(tc.tile_pool(name="w_v", bufs=8))
+        w_pool = ctx.enter_context(tc.tile_pool(name="w", bufs=8))
         result = ctx.enter_context(tc.tile_pool(name="result", bufs=2))
         psum_acc = ctx.enter_context(tc.psum_pool(name="psum_acc", bufs=1))
         psum_work = ctx.enter_context(tc.psum_pool(name="psum_work", bufs=2))
@@ -84,8 +85,8 @@ def tile_qwenblock_pa_k_kernel(
         nc.scalar.activation(out=warm_col[:], in_=one_col[:], func=ACT.Sqrt)
 
         h_flat = hidden_states.flatten_outer_dims()
-        for c in range(D // X_CHUNK):
-            cols = slice(c * X_CHUNK, (c + 1) * X_CHUNK)
+        for c in range(D // X_LOAD):
+            cols = slice(c * X_LOAD, (c + 1) * X_LOAD)
             nc.sync.dma_start(out=h_sb[:, cols], in_=h_flat[:, cols])
         nc.scalar.dma_start(out=g1_rows[0:GROUPS, :], in_=g1.rearrange("(g c) -> g c", c=K_PASS))
         nc.scalar.dma_start(out=bias_rows[0:1, :], in_=bqkv.rearrange("(o n) -> o n", o=1))
@@ -152,8 +153,8 @@ def tile_qwenblock_pa_k_kernel(
                 in_=grouped[:].rearrange("p m t -> p (m t)"),
             )
 
-        def load_columns(pool, g, first_col, cols):
-            words = pool.tile([P, cols], U32, align_bytes=64, tag="words")
+        def load_columns(g, first_col, cols):
+            words = w_pool.tile([P, cols], U32, align_bytes=64, tag="words")
             byte_cols = slice(first_col * PACK, (first_col + cols) * PACK)
             nc.sync.dma_start(
                 out=words[:].bitcast(I32),
@@ -161,20 +162,23 @@ def tile_qwenblock_pa_k_kernel(
             )
             return words
 
-        def load_words(pool, g, first_bank, banks):
-            return load_columns(pool, g, first_bank * BANK, banks * BANK)
+        def load_words(g, first_bank, banks):
+            return load_columns(g, first_bank * BANK, banks * BANK)
 
-        def multiply(g, words, first_bank, banks, skip=0, last_group=GROUPS - 1):
+        last = GROUPS - 1
+        bank_a, bank_b = QK_BANKS, QK_BANKS + 1
+
+        def multiply(g, words, first_bank, banks):
             for i in range(banks):
                 b = first_bank + i
                 nc.tensor.matmul_mx(
                     out=acc[b][:],
                     lhsT=x_codes[:, g, :].bitcast(FP8X4),
                     lhsT_scale=x_planes[:, g, :],
-                    rhs=words[:, (skip + i) * BANK : (skip + i + 1) * BANK].bitcast(FP8X4),
+                    rhs=words[:, i * BANK : (i + 1) * BANK].bitcast(FP8X4),
                     rhs_scale=w_planes[4 * (g % SHARE) : P, g // SHARE, b * BANK : (b + 1) * BANK],
                     start=(g == 0),
-                    stop=(g == last_group),
+                    stop=(g == (last - 1 if b == bank_b else last)),
                 )
 
         def rope_and_store(first_bank, out):
@@ -210,25 +214,23 @@ def tile_qwenblock_pa_k_kernel(
         for g in range(AHEAD):
             quantise_x(g)
         for g in range(GROUPS):
-            words = load_words(w_qk_pool, g, 0, QK_BANKS)
-            multiply(g, words, 0, QK_BANKS)
+            banks = QK_BANKS + V_BANKS if g < FULL_GROUPS else QK_BANKS
+            words = load_words(g, 0, banks)
+            multiply(g, words, 0, banks)
             if g + AHEAD < GROUPS:
                 quantise_x(g + AHEAD)
         q_sb = rope_and_store(0, out_0)
         k_sb = rope_and_store(PART // BANK, out_1)
 
-        last = GROUPS - 1
-        bank_a, bank_b = QK_BANKS, QK_BANKS + 1
-        for g in range(last):
-            words = load_words(w_v_pool, g, QK_BANKS, V_BANKS)
-            multiply(g, words, bank_a, 1)
-            multiply(g, words, bank_b, 1, skip=1, last_group=last - 1)
-        words = load_words(w_v_pool, last, bank_a, 1)
+        for g in range(FULL_GROUPS, last):
+            words = load_words(g, QK_BANKS, V_BANKS)
+            multiply(g, words, QK_BANKS, V_BANKS)
+        words = load_words(last, bank_a, 1)
         multiply(last, words, bank_a, 1)
         late = []
         for i in range(BANK // TAIL):
             first_col = bank_b * BANK + i * TAIL
-            words = load_columns(w_v_pool, last, first_col, TAIL)
+            words = load_columns(last, first_col, TAIL)
             late_ps = psum_work.tile([P, TAIL], F32, tag="work")
             nc.tensor.matmul_mx(
                 out=late_ps[:],

@@ -29,7 +29,6 @@ X_CHUNK = 2048
 X_LOAD = 4096
 SHARE = 4
 AHEAD = 4
-TAIL = 256
 FULL_GROUPS = 6
 EPS = 1e-6
 
@@ -165,9 +164,6 @@ def tile_qwenblock_pa_k_kernel(
         def load_words(g, first_bank, banks):
             return load_columns(g, first_bank * BANK, banks * BANK)
 
-        last = GROUPS - 1
-        bank_a, bank_b = QK_BANKS, QK_BANKS + 1
-
         def multiply(g, words, first_bank, banks):
             for i in range(banks):
                 b = first_bank + i
@@ -178,7 +174,7 @@ def tile_qwenblock_pa_k_kernel(
                     rhs=words[:, i * BANK : (i + 1) * BANK].bitcast(FP8X4),
                     rhs_scale=w_planes[4 * (g % SHARE) : P, g // SHARE, b * BANK : (b + 1) * BANK],
                     start=(g == 0),
-                    stop=(g == (last - 1 if b == bank_b else last)),
+                    stop=(g == GROUPS - 1),
                 )
 
         def rope_and_store(first_bank, out):
@@ -222,37 +218,16 @@ def tile_qwenblock_pa_k_kernel(
         q_sb = rope_and_store(0, out_0)
         k_sb = rope_and_store(PART // BANK, out_1)
 
-        for g in range(FULL_GROUPS, last):
+        for g in range(FULL_GROUPS, GROUPS):
             words = load_words(g, QK_BANKS, V_BANKS)
             multiply(g, words, QK_BANKS, V_BANKS)
-        words = load_words(last, bank_a, 1)
-        multiply(last, words, bank_a, 1)
-        late = []
-        for i in range(BANK // TAIL):
-            first_col = bank_b * BANK + i * TAIL
-            words = load_columns(last, first_col, TAIL)
-            late_ps = psum_work.tile([P, TAIL], F32, tag="work")
-            nc.tensor.matmul_mx(
-                out=late_ps[:],
-                lhsT=x_codes[:, last, :].bitcast(FP8X4),
-                lhsT_scale=x_planes[:, last, :],
-                rhs=words[:].bitcast(FP8X4),
-                rhs_scale=w_planes[4 * (last % SHARE) : P, last // SHARE, first_col : first_col + TAIL],
-                start=True,
-                stop=True,
-            )
-            late.append(late_ps)
         nc.sync.dma_start(out=out_0.rearrange("b s h d -> (b s) h d"), in_=q_sb[:])
         nc.sync.dma_start(out=out_1.rearrange("b s h d -> (b s) h d"), in_=k_sb[:])
         v_flat = out_2.rearrange("b s h d -> (b s) (h d)")
-        v_sb = {}
-        for b in (bank_b, bank_a):
-            v_sb[b] = result.tile([P, BANK], F32, name="v_sb%d" % b)
+        for i in range(V_BANKS):
+            b = QK_BANKS + i
+            v_sb = result.tile([P, BANK], F32)
             nc.vector.tensor_tensor(
-                out=v_sb[b][:], in0=acc[b][:], in1=bias_all[:, b * BANK : (b + 1) * BANK], op=ALU.add
+                out=v_sb[:], in0=acc[b][:], in1=bias_all[:, b * BANK : (b + 1) * BANK], op=ALU.add
             )
-        nc.sync.dma_start(out=v_flat[:, 0:BANK], in_=v_sb[bank_a][:])
-        for i in range(BANK // TAIL):
-            cols = slice(i * TAIL, (i + 1) * TAIL)
-            nc.vector.tensor_tensor(out=v_sb[bank_b][:, cols], in0=late[i][:], in1=v_sb[bank_b][:, cols], op=ALU.add)
-            nc.sync.dma_start(out=v_flat[:, BANK + i * TAIL : BANK + (i + 1) * TAIL], in_=v_sb[bank_b][:, cols])
+            nc.sync.dma_start(out=v_flat[:, i * BANK : (i + 1) * BANK], in_=v_sb[:])

@@ -40,7 +40,7 @@ def tile_qwenblock_pa_k_kernel(
 ):
     nc = tc.nc
     with ExitStack() as ctx:
-        ctx.enter_context(tc.manual_schedule())
+        ctx.enter_context(tc.manual_schedule(engines={mybir.EngineType.SP}))
         keep = ctx.enter_context(tc.tile_pool(name="keep", bufs=1))
         squares = ctx.enter_context(tc.tile_pool(name="squares", bufs=2))
         stage = ctx.enter_context(tc.tile_pool(name="stage", bufs=3))

from contextlib import ExitStack

import concourse.masks as masks
import concourse.mybir as mybir

F32 = mybir.dt.float32
BF16 = mybir.dt.bfloat16
I32 = mybir.dt.int32
U32 = mybir.dt.uint32
U8 = mybir.dt.uint8
FP8X4 = mybir.dt.float8_e4m3fn_x4
ALU = mybir.AluOpType
ACT = mybir.ActivationFunctionType

P = 128
PACK = 4
K_PASS = P * PACK
D = 8192
GROUPS = D // K_PASS
HEADS = 8
HEAD_DIM = 128
HALF = HEAD_DIM // 2
PART = HEADS * HEAD_DIM
N_OUT = 3 * PART
BANK = 512
QK_BANKS = 2 * PART // BANK
V_BANKS = PART // BANK
X_CHUNK = 2048
X_LOAD = 4096
SHARE = 4
AHEAD = 4
FULL_GROUPS = 6
EPS = 1e-6

FLOPS = 2 * P * D * N_OUT


def tile_qwenblock_pa_k_kernel(
    tc, hidden_states, cos, sin, g1, Wqkv_words, Wqkv_scales, bqkv, out_0, out_1, out_2
):
    nc = tc.nc
    with ExitStack() as ctx:
        ctx.enter_context(tc.manual_schedule(engines={mybir.EngineType.SP}))
        keep = ctx.enter_context(tc.tile_pool(name="keep", bufs=1))
        squares = ctx.enter_context(tc.tile_pool(name="squares", bufs=2))
        stage = ctx.enter_context(tc.tile_pool(name="stage", bufs=3))
        quant = ctx.enter_context(tc.tile_pool(name="quant", bufs=3))
        w_pool = ctx.enter_context(tc.tile_pool(name="w", bufs=8))
        result = ctx.enter_context(tc.tile_pool(name="result", bufs=2))
        psum_acc = ctx.enter_context(tc.psum_pool(name="psum_acc", bufs=1))
        psum_work = ctx.enter_context(tc.psum_pool(name="psum_work", bufs=2))

        h_sb = keep.tile([P, D], BF16)
        g1_rows = keep.tile([P, K_PASS], BF16)
        g1_sorted = keep.tile([P, PACK, P], BF16)
        g1_t = keep.tile([P, GROUPS, PACK], F32)
        bias_rows = keep.tile([P, N_OUT], BF16)
        bias_all = keep.tile([P, N_OUT], F32)
        cos_sb = keep.tile([P, HEAD_DIM], BF16)
        sin_sb = keep.tile([P, HEAD_DIM], BF16)
        sin_signed = keep.tile([P, HEAD_DIM], BF16)
        ident_f32 = keep.tile([P, P], F32)
        ident_bf16 = keep.tile([P, P], BF16)
        ones_bf16 = keep.tile([P, P], BF16)
        one_col = keep.tile([P, 1], F32)
        warm_col = keep.tile([P, 1], F32)
        sum_sq = keep.tile([P, D // X_CHUNK], F32)
        sum_sq_all = keep.tile([P, 1], F32)
        mean_sq = keep.tile([P, 1], F32)
        rms = keep.tile([P, 1], F32)
        inv_rms = keep.tile([P, 1], F32)
        x_codes = keep.tile([P, GROUPS, P], U32, align_bytes=64)
        x_planes = keep.tile([P, GROUPS, P], U8, align_bytes=64)
        w_planes = keep.tile([P, GROUPS // SHARE, N_OUT], U8, align_bytes=64)
        acc = [psum_acc.tile([P, BANK], F32, name="acc%d" % b) for b in range(QK_BANKS + V_BANKS)]

        nc.vector.memset(one_col[:], 1.0)
        nc.vector.memset(g1_rows[:], 0.0)
        nc.vector.memset(bias_rows[:], 0.0)
        nc.vector.memset(w_planes[:].bitcast(I32), 0)
        masks.make_identity(nc, ident_bf16[:])
        masks.make_identity(nc, ident_f32[:])
        nc.gpsimd.memset(ones_bf16[:], 1.0)
        nc.scalar.activation(out=warm_col[:], in_=one_col[:], func=ACT.Sqrt)

        h_flat = hidden_states.flatten_outer_dims()
        for c in range(D // X_LOAD):
            cols = slice(c * X_LOAD, (c + 1) * X_LOAD)
            nc.sync.dma_start(out=h_sb[:, cols], in_=h_flat[:, cols])
        nc.scalar.dma_start(out=g1_rows[0:GROUPS, :], in_=g1.rearrange("(g c) -> g c", c=K_PASS))
        nc.scalar.dma_start(out=bias_rows[0:1, :], in_=bqkv.rearrange("(o n) -> o n", o=1))
        nc.scalar.dma_start(out=cos_sb[:], in_=cos.rearrange("b s o d -> (b s o) d"))
        nc.scalar.dma_start(out=sin_sb[:], in_=sin.rearrange("b s o d -> (b s o) d"))
        for j in range(GROUPS // SHARE):
            for quadrant in range(4):
                nc.gpsimd.dma_start(
                    out=w_planes[32 * quadrant : 32 * quadrant + 4 * SHARE, j, :].bitcast(F32),
                    in_=Wqkv_scales[
                        SHARE * j : SHARE * (j + 1), 4 * quadrant : 4 * quadrant + 4, :
                    ].bitcast(F32),
                )

        nc.vector.tensor_copy(out=g1_sorted[:], in_=g1_rows[:].rearrange("r (p t) -> r t p", t=PACK))
        g1_ps = psum_work.tile([P, PACK, P], BF16, tag="work")
        for t in range(PACK):
            nc.tensor.transpose(g1_ps[:, t, :], g1_sorted[:, t, :], ident_bf16[:])
        nc.vector.tensor_copy(out=g1_t[:], in_=g1_ps[:, :, 0:GROUPS].rearrange("p t g -> p g t"))

        for b in range(QK_BANKS + V_BANKS):
            cols = slice(b * BANK, (b + 1) * BANK)
            bias_ps = psum_work.tile([P, BANK], F32, tag="work")
            nc.tensor.matmul(out=bias_ps[:], lhsT=ones_bf16[:], rhs=bias_rows[:, cols], start=True, stop=True)
            nc.vector.tensor_copy(out=bias_all[:, cols], in_=bias_ps[:])

        nc.vector.tensor_scalar_mul(out=sin_signed[:, 0:HALF], in0=sin_sb[:, 0:HALF], scalar1=-1.0)
        nc.vector.tensor_copy(out=sin_signed[:, HALF:HEAD_DIM], in_=sin_sb[:, HALF:HEAD_DIM])

        for c in range(D // X_CHUNK):
            cols = slice(c * X_CHUNK, (c + 1) * X_CHUNK)
            squared = squares.tile([P, X_CHUNK], BF16)
            nc.scalar.activation(
                out=squared[:], in_=h_sb[:, cols], func=ACT.Square, accum_out=sum_sq[:, c : c + 1]
            )
        nc.vector.tensor_reduce(out=sum_sq_all[:], in_=sum_sq[:], axis=mybir.AxisListType.X, op=ALU.add)
        nc.vector.tensor_scalar(
            out=mean_sq[:], in0=sum_sq_all[:], scalar1=1.0 / D, scalar2=EPS, op0=ALU.mult, op1=ALU.add
        )
        nc.scalar.activation(out=rms[:], in_=mean_sq[:], func=ACT.Sqrt)
        nc.vector.reciprocal(out=inv_rms[:], in_=rms[:])

        def quantise_x(g):
            scaled = stage.tile([P, PACK, P], F32)
            nc.scalar.activation(
                out=scaled[:],
                in_=h_sb[:, g * K_PASS : (g + 1) * K_PASS].rearrange("m (p t) -> m t p", t=PACK),
                func=ACT.Copy,
                scale=inv_rms[:, 0:1],
            )
            turned = psum_work.tile([P, PACK, P], F32, tag="work")
            for t in range(PACK):
                nc.tensor.transpose(turned[:, t, :], scaled[:, t, :], ident_f32[:])
            grouped = quant.tile([P, P, PACK], BF16, align_bytes=64)
            nc.vector.tensor_tensor(
                out=grouped[:],
                in0=turned[:].rearrange("p t m -> p m t"),
                in1=g1_t[:, g, :].unsqueeze(1).to_broadcast([P, P, PACK]),
                op=ALU.mult,
            )
            nc.vector.quantize_mx(
                out=x_codes[:, g, :].bitcast(FP8X4),
                scales=x_planes[:, g, :],
                in_=grouped[:].rearrange("p m t -> p (m t)"),
            )

        def load_columns(g, first_col, cols):
            words = w_pool.tile([P, cols], U32, align_bytes=64, tag="words")
            byte_cols = slice(first_col * PACK, (first_col + cols) * PACK)
            nc.sync.dma_start(
                out=words[:].bitcast(I32),
                in_=Wqkv_words[g].rearrange("p n t -> p (n t)")[:, byte_cols].bitcast(I32),
            )
            return words

        def load_words(g, first_bank, banks):
            return load_columns(g, first_bank * BANK, banks * BANK)

        def multiply(g, words, first_bank, banks):
            for i in range(banks):
                b = first_bank + i
                nc.tensor.matmul_mx(
                    out=acc[b][:],
                    lhsT=x_codes[:, g, :].bitcast(FP8X4),
                    lhsT_scale=x_planes[:, g, :],
                    rhs=words[:, i * BANK : (i + 1) * BANK].bitcast(FP8X4),
                    rhs_scale=w_planes[4 * (g % SHARE) : P, g // SHARE, b * BANK : (b + 1) * BANK],
                    start=(g == 0),
                    stop=(g == GROUPS - 1),
                )

        def rope_and_store(first_bank, out):
            u = result.tile([P, HEADS, HEAD_DIM], F32)
            swapped = result.tile([P, HEADS, HEAD_DIM], F32)
            heads_in_bank = BANK // HEAD_DIM
            for i in range(PART // BANK):
                b = first_bank + i
                nc.vector.tensor_tensor(
                    out=u[:, i * heads_in_bank : (i + 1) * heads_in_bank, :],
                    in0=acc[b][:].rearrange("m (h d) -> m h d", d=HEAD_DIM),
                    in1=bias_all[:, b * BANK : (b + 1) * BANK].rearrange("m (h d) -> m h d", d=HEAD_DIM),
                    op=ALU.add,
                )
            nc.vector.tensor_tensor(
                out=swapped[:, :, 0:HALF],
                in0=u[:, :, HALF:HEAD_DIM],
                in1=sin_signed[:, 0:HALF].unsqueeze(1).to_broadcast([P, HEADS, HALF]),
                op=ALU.mult,
            )
            nc.vector.tensor_tensor(
                out=swapped[:, :, HALF:HEAD_DIM],
                in0=u[:, :, 0:HALF],
                in1=sin_signed[:, HALF:HEAD_DIM].unsqueeze(1).to_broadcast([P, HEADS, HALF]),
                op=ALU.mult,
            )
            nc.vector.tensor_tensor(
                out=u[:], in0=u[:], in1=cos_sb[:].unsqueeze(1).to_broadcast([P, HEADS, HEAD_DIM]), op=ALU.mult
            )
            nc.vector.tensor_tensor(out=u[:], in0=u[:], in1=swapped[:], op=ALU.add)
            return u

        for g in range(AHEAD):
            quantise_x(g)
        for g in range(GROUPS):
            banks = QK_BANKS + V_BANKS if g < FULL_GROUPS else QK_BANKS
            words = load_words(g, 0, banks)
            multiply(g, words, 0, banks)
            if g + AHEAD < GROUPS:
                quantise_x(g + AHEAD)
        q_sb = rope_and_store(0, out_0)
        k_sb = rope_and_store(PART // BANK, out_1)

        for g in range(FULL_GROUPS, GROUPS):
            words = load_words(g, QK_BANKS, V_BANKS)
            multiply(g, words, QK_BANKS, V_BANKS)
        nc.sync.dma_start(out=out_0.rearrange("b s h d -> (b s) h d"), in_=q_sb[:])
        nc.sync.dma_start(out=out_1.rearrange("b s h d -> (b s) h d"), in_=k_sb[:])
        v_flat = out_2.rearrange("b s h d -> (b s) (h d)")
        for i in range(V_BANKS):
            b = QK_BANKS + i
            v_sb = result.tile([P, BANK], F32)
            nc.vector.tensor_tensor(
                out=v_sb[:], in0=acc[b][:], in1=bias_all[:, b * BANK : (b + 1) * BANK], op=ALU.add
            )
            nc.sync.dma_start(out=v_flat[:, i * BANK : (i + 1) * BANK], in_=v_sb[:])
